import numpy as np
import ml_dtypes


def mxq(x, axis, fmt="e4m3"):
    dtype, down = {"e4m3": (ml_dtypes.float8_e4m3fn, 7), "e5m2": (ml_dtypes.float8_e5m2, 14)}[fmt]
    v = np.moveaxis(np.asarray(x, np.float32).astype(ml_dtypes.bfloat16).astype(np.float64), axis, -1)
    blocks = v.reshape(v.shape[:-1] + (-1, 32))
    amax = np.abs(blocks).max(-1, keepdims=True)
    byte = np.maximum(np.where(amax > 0, np.frexp(amax)[1] - 1 + 127, 0) - down, 1)
    scale = np.exp2(byte - 127.0)
    codes = (blocks / scale).astype(np.float32).astype(dtype).astype(np.float64)
    return np.moveaxis((codes * scale).reshape(v.shape), -1, axis)


WIDE = False


def mx_kscale(k):
    if not WIDE:
        return np.ones(k)
    levels = np.array([10, -10, 5, -5, 0])
    a = np.random.permutation(np.resize(levels, k // 512 * 4)).reshape(k // 512, 4)
    idx = np.arange(k)
    return np.exp2(a[idx // 512, idx % 128 // 32])


BF16 = ml_dtypes.bfloat16


def bf(x):
    return np.asarray(x, np.float32).astype(BF16)


def f64(x):
    return np.asarray(x).astype(np.float64)


E2M1 = np.array([0.0, 0.5, 1.0, 1.5, 2.0, 3.0, 4.0, 6.0, -0.0, -0.5, -1.0, -1.5, -2.0, -3.0, -4.0, -6.0])


def pack_weight(w, fmt):
    k, n = w.shape
    w = f64(bf(w)).reshape(k // 32, 32, n)
    amax = np.abs(w).max(1)
    if fmt == "e4m3":
        byte = np.frexp(amax)[1] - 1 + 127 - 7
    else:
        mant, ex = np.frexp(amax / 6.0)
        byte = np.where(mant > 0.5, ex, ex - 1) + 127
    byte = np.clip(np.where(amax > 0, byte, 1), 1, 254)
    scaled = (w * np.exp2(127.0 - byte)[:, None, :]).reshape(k, n).astype(np.float32)
    by_word = np.ascontiguousarray(scaled.reshape(k // 512, 128, 4, n).transpose(0, 1, 3, 2))
    if fmt == "e4m3":
        words = by_word.astype(ml_dtypes.float8_e4m3fn).view(np.uint8)
    else:
        c = by_word.astype(ml_dtypes.float4_e2m1fn).view(np.uint8) & 0xF
        words = c[..., 0::2] | (c[..., 1::2] << 4)
    return np.ascontiguousarray(words), np.ascontiguousarray(byte.astype(np.uint8).reshape(k // 512, 16, n))


def unpack_weight(words, scales, fmt):
    g, p, n, _ = words.shape
    if fmt == "e4m3":
        vals = np.ascontiguousarray(words).view(ml_dtypes.float8_e4m3fn).astype(np.float64)
    else:
        nib = np.empty((g, p, n, 4), np.uint8)
        nib[..., 0::2] = words & 0xF
        nib[..., 1::2] = words >> 4
        vals = E2M1[nib]
    vals = vals * np.repeat(np.exp2(scales.astype(np.float64) - 127.0), 8, axis=1)[..., None]
    return vals.transpose(0, 1, 3, 2).reshape(g * 512, n)


B, NV, NH, NT = 128, 8192, 2048, 2
FMT = "e4m3"


def softplus(v):
    return np.logaddexp(v, 0.0)


def softmax_last(v):
    e = np.exp(v - v.max(axis=1, keepdims=True))
    return e / e.sum(axis=1, keepdims=True)


def setup_inputs():
    s = mx_kscale(NV)
    input_data = bf(np.random.standard_normal((B, NV)) * s)
    w = np.random.standard_normal((NH, NV)) / np.sqrt(NV) / s[None, :]
    words, scales = pack_weight(np.ascontiguousarray(w.T), FMT)
    return {"input_data": input_data,
            "W_words": words,
            "W_scales": scales,
            "U": bf(np.random.standard_normal((NH, NT)) * 0.5),
            "h_bias": bf(np.random.standard_normal((1, NH)) * 0.5 - np.log(NH / 16.0)),
            "y_bias": bf(np.random.standard_normal((1, NT)) * 0.5)}


def reference(input_data, W_words, W_scales, U, h_bias, y_bias):
    pf = (mxq(f64(input_data), 1, "e4m3") @ unpack_weight(W_words, W_scales, FMT)) + f64(h_bias)
    sp = softplus(pf[:, :, None] + f64(U)[None, :, :])
    logits = f64(y_bias) + sp.sum(axis=1)
    return softmax_last(logits)

@@ -1,0 +1,192 @@
+from contextlib import ExitStack
+
+import concourse.mybir as mybir
+from concourse.masks import make_identity
+
+F32 = mybir.dt.float32
+BF16 = mybir.dt.bfloat16
+I32 = mybir.dt.int32
+U32 = mybir.dt.uint32
+U8 = mybir.dt.uint8
+FP8X4 = mybir.dt.float8_e4m3fn_x4
+ACT = mybir.ActivationFunctionType
+ALU = mybir.AluOpType
+
+P = 128
+BATCH = 128
+VISIBLE = 8192
+HIDDEN = 2048
+CLASSES = 2
+PACK = 4
+K_PASS = P * PACK
+GROUPS = VISIBLE // K_PASS
+TILES = HIDDEN // P
+PLANES = 4
+QUADRANTS = 4
+
+RANGE_TILES = (7, 7, 2)
+GROUPS_PER_LOAD = 2
+X_CHUNK_GROUPS = 4
+BANK_GROUPS = 2
+
+FLOPS = 2 * BATCH * VISIBLE * HIDDEN
+
+assert sum(RANGE_TILES) == TILES
+
+
+def tile_rbm_w_kernel(tc, input_data, W_words, W_scales, U, h_bias, y_bias, out):
+    nc = tc.nc
+    with ExitStack() as ctx:
+        keep = ctx.enter_context(tc.tile_pool(name="keep", bufs=1))
+        work = ctx.enter_context(tc.tile_pool(name="work", bufs=4))
+        psum = ctx.enter_context(tc.psum_pool(name="psum", bufs=8))
+
+        chunk_cols = X_CHUNK_GROUPS * K_PASS
+        x_chunks = []
+        for j in range(GROUPS // X_CHUNK_GROUPS):
+            x_sb = keep.tile([P, chunk_cols], BF16, name="x_sb%d" % j)
+            nc.sync.dma_start(out=x_sb[:], in_=input_data[:, j * chunk_cols : (j + 1) * chunk_cols])
+            x_chunks.append(x_sb)
+
+        w_planes = keep.tile([P, GROUPS // PLANES, HIDDEN], U8, align_bytes=64)
+        nc.vector.memset(w_planes[:].rearrange("p a n -> p (a n)").bitcast(I32), 0)
+        for a in range(GROUPS // PLANES):
+            for q in range(QUADRANTS):
+                nc.sync.dma_start(
+                    out=w_planes[32 * q : 32 * q + 4 * PLANES, a, :].bitcast(I32),
+                    in_=W_scales[PLANES * a : PLANES * (a + 1), 4 * q : 4 * q + 4, :].bitcast(I32),
+                )
+
+        w_loads = []
+        first_tile = 0
+        for r, tiles in enumerate(RANGE_TILES):
+            byte0 = first_tile * P * PACK
+            byte1 = (first_tile + tiles) * P * PACK
+            loads = []
+            for l in range(GROUPS // GROUPS_PER_LOAD):
+                w_sb = keep.tile([P, GROUPS_PER_LOAD, tiles * P], U32, name="w_sb%d_%d" % (r, l), align_bytes=64)
+                groups = W_words[l * GROUPS_PER_LOAD : (l + 1) * GROUPS_PER_LOAD]
+                nc.sync.dma_start(
+                    out=w_sb[:].bitcast(I32),
+                    in_=groups.rearrange("g p n t -> p g (n t)")[:, :, byte0:byte1].bitcast(I32),
+                )
+                loads.append(w_sb)
+            w_loads.append(loads)
+            first_tile += tiles
+
+        rows_bf = keep.tile([P, (1 + CLASSES) * P], BF16)
+        nc.vector.memset(rows_bf[:], 0.0)
+        nc.scalar.dma_start(out=rows_bf[0:TILES, 0:P], in_=h_bias.rearrange("o (t p) -> (o t) p", p=P))
+        nc.scalar.dma_start(out=rows_bf[0:TILES, P:], in_=U.rearrange("(t p) c -> t (p c)", p=P))
+        y_sb = keep.tile([P, CLASSES], BF16)
+        nc.scalar.dma_start(out=y_sb[:], in_=y_bias.rearrange("o c -> (o c)").partition_broadcast(P))
+
+        ident = keep.tile([P, P], F32)
+        make_identity(nc, ident[:])
+        ones = keep.tile([P, P], F32)
+        nc.vector.memset(ones[:], 1.0)
+
+        x_codes = keep.tile([P, GROUPS * BATCH], U32, align_bytes=64)
+        x_scales = keep.tile([P, GROUPS * BATCH], U8, align_bytes=64)
+        words = K_PASS // 2
+        for j, x_sb in enumerate(x_chunks):
+            x_words = x_sb[:].bitcast(F32)
+            grouped = keep.tile([P, chunk_cols], BF16, name="grouped%d" % j, align_bytes=64)
+            for h in range(X_CHUNK_GROUPS // BANK_GROUPS):
+                turned = psum.tile([P, BANK_GROUPS, 2, BATCH], F32, tag="bank")
+                for g in range(BANK_GROUPS):
+                    word0 = (h * BANK_GROUPS + g) * words
+                    for u in range(2):
+                        nc.tensor.transpose(turned[:, g, u, :], x_words[:, word0 + u : word0 + words : 2], ident[:])
+                half = BANK_GROUPS * words
+                dst = grouped[:].bitcast(F32)[:, h * half : (h + 1) * half]
+                dst = dst.rearrange("p (g b u) -> p g b u", g=BANK_GROUPS, u=2)
+                src = turned[:].rearrange("p g u b -> p g b u")
+                if h % 2 == 0:
+                    nc.vector.tensor_copy(out=dst, in_=src)
+                else:
+                    nc.scalar.copy(out=dst, in_=src)
+            cols = slice(j * X_CHUNK_GROUPS * BATCH, (j + 1) * X_CHUNK_GROUPS * BATCH)
+            nc.vector.quantize_mx(out=x_codes[:, cols].bitcast(FP8X4), scales=x_scales[:, cols], in_=grouped[:])
+
+        u_rows = rows_bf[:, P:].rearrange("r (p c) -> r p c", c=CLASSES)
+        rows = keep.tile([P, 1 + CLASSES, P], F32)
+        for c in range(CLASSES):
+            nc.vector.tensor_tensor(out=rows[:, c, :], in0=rows_bf[:, 0:P], in1=u_rows[:, :, c], op=ALU.add)
+        nc.vector.tensor_tensor(out=rows[:, CLASSES, :], in0=u_rows[:, :, 0], in1=u_rows[:, :, 1], op=ALU.subtract)
+        rows_turned = psum.tile([P, 1 + CLASSES, P], F32, tag="bank")
+        for i in range(1 + CLASSES):
+            nc.tensor.transpose(rows_turned[:, i, :], rows[:, i, :], ident[:])
+        per_unit = keep.tile([P, 1 + CLASSES, TILES], F32)
+        nc.vector.tensor_copy(out=per_unit[:], in_=rows_turned[:, :, 0:TILES])
+        y_diff = keep.tile([P, CLASSES], F32)
+        for c in range(CLASSES):
+            nc.vector.tensor_sub(out=y_diff[:, c : c + 1], in0=y_sb[:, c : c + 1], in1=y_sb[:, 1 - c : 2 - c])
+
+        factors = keep.tile([P, CLASSES, BATCH], F32)
+        nc.vector.memset(factors[:], 1.0)
+        relu2 = keep.tile([P, BATCH], F32)
+        nc.vector.memset(relu2[:], 0.0)
+
+        first_tile = 0
+        for r, tiles in enumerate(RANGE_TILES):
+            accs = [psum.tile([P, BATCH], F32, tag="bank", name="acc%d" % (first_tile + i)) for i in range(tiles)]
+            for g in range(GROUPS):
+                w_sb = w_loads[r][g // GROUPS_PER_LOAD]
+                plane_start = 4 * (g % PLANES)
+                for i in range(tiles):
+                    t = first_tile + i
+                    nc.tensor.matmul_mx(
+                        out=accs[i][:],
+                        lhsT=w_sb[:, g % GROUPS_PER_LOAD, i * P : (i + 1) * P].bitcast(FP8X4),
+                        lhsT_scale=w_planes[plane_start:P, g // PLANES, t * P : (t + 1) * P],
+                        rhs=x_codes[:, g * BATCH : (g + 1) * BATCH].bitcast(FP8X4),
+                        rhs_scale=x_scales[:, g * BATCH : (g + 1) * BATCH],
+                        start=(g == 0),
+                        stop=(g == GROUPS - 1),
+                    )
+            for i in range(tiles):
+                t = first_tile + i
+                mag = work.tile([P, CLASSES, BATCH], F32)
+                for c in range(CLASSES):
+                    nc.scalar.activation(
+                        out=mag[:, c, :], in_=accs[i][:], func=ACT.Abs, bias=per_unit[:, c, t : t + 1], scale=1.0
+                    )
+                decay = work.tile([P, CLASSES, BATCH], F32)
+                nc.scalar.activation(out=decay[:], in_=mag[:], func=ACT.Exp, scale=-1.0)
+                nc.vector.scalar_tensor_tensor(
+                    out=factors[:], in0=decay[:], scalar=1.0, in1=factors[:], op0=ALU.add, op1=ALU.mult
+                )
+                nc.vector.scalar_tensor_tensor(
+                    out=relu2[:],
+                    in0=mag[:, 0, :],
+                    scalar=per_unit[:, CLASSES, t : t + 1],
+                    in1=relu2[:],
+                    op0=ALU.add,
+                    op1=ALU.add,
+                )
+                nc.vector.tensor_sub(out=relu2[:], in0=relu2[:], in1=mag[:, 1, :])
+            first_tile += tiles
+
+        logs = keep.tile([P, CLASSES, BATCH], F32)
+        nc.scalar.activation(out=logs[:], in_=factors[:], func=ACT.Ln)
+        log_diff = keep.tile([P, BATCH], F32)
+        nc.vector.tensor_sub(out=log_diff[:], in0=logs[:, 0, :], in1=logs[:, 1, :])
+        partial = keep.tile([P, BATCH], F32)
+        nc.vector.scalar_tensor_tensor(
+            out=partial[:], in0=relu2[:], scalar=0.5, in1=log_diff[:], op0=ALU.mult, op1=ALU.add
+        )
+        logit_diff = psum.tile([P, BATCH], F32, tag="bank")
+        nc.tensor.matmul(out=logit_diff[:], lhsT=ones[:], rhs=partial[:], start=True, stop=True)
+        probs = keep.tile([P, BATCH, CLASSES], F32)
+        for c in range(CLASSES):
+            nc.scalar.activation(
+                out=probs[:, :, c],
+                in_=logit_diff[:],
+                func=ACT.Sigmoid,
+                bias=y_diff[:, c : c + 1],
+                scale=1.0 - 2.0 * c,
+            )
+        nc.sync.dma_start(
+            out=out.rearrange("(o b) c -> o (b c)", o=1), in_=probs[0:1, :, :].rearrange("o b c -> o (b c)")
+        )

@@ -24,7 +24,7 @@ TILES = HIDDEN // P
 PLANES = 4
 QUADRANTS = 4
 
-RANGE_TILES = (7, 7, 2)
+RANGE_TILES = (8, 6, 2)
 GROUPS_PER_LOAD = 2
 X_CHUNK_GROUPS = 4
 BANK_GROUPS = 2
@@ -40,6 +40,7 @@ def tile_rbm_w_kernel(tc, input_data, W_words, W_scales, U, h_bias, y_bias, out)
         keep = ctx.enter_context(tc.tile_pool(name="keep", bufs=1))
         work = ctx.enter_context(tc.tile_pool(name="work", bufs=4))
         psum = ctx.enter_context(tc.psum_pool(name="psum", bufs=8))
+        ctx.enter_context(tc.manual_schedule())
 
         chunk_cols = X_CHUNK_GROUPS * K_PASS
         x_chunks = []
@@ -50,7 +51,8 @@ def tile_rbm_w_kernel(tc, input_data, W_words, W_scales, U, h_bias, y_bias, out)
 
         w_planes = keep.tile([P, GROUPS // PLANES, HIDDEN], U8, align_bytes=64)
         nc.vector.memset(w_planes[:].rearrange("p a n -> p (a n)").bitcast(I32), 0)
-        for a in range(GROUPS // PLANES):
+
+        def load_scale_block(a):
             for q in range(QUADRANTS):
                 nc.sync.dma_start(
                     out=w_planes[32 * q : 32 * q + 4 * PLANES, a, :].bitcast(I32),
@@ -64,6 +66,8 @@ def tile_rbm_w_kernel(tc, input_data, W_words, W_scales, U, h_bias, y_bias, out)
             byte1 = (first_tile + tiles) * P * PACK
             loads = []
             for l in range(GROUPS // GROUPS_PER_LOAD):
+                if r == 0 and (l * GROUPS_PER_LOAD) % PLANES == 0:
+                    load_scale_block(l * GROUPS_PER_LOAD // PLANES)
                 w_sb = keep.tile([P, GROUPS_PER_LOAD, tiles * P], U32, name="w_sb%d_%d" % (r, l), align_bytes=64)
                 groups = W_words[l * GROUPS_PER_LOAD : (l + 1) * GROUPS_PER_LOAD]
                 nc.sync.dma_start(
@@ -79,19 +83,30 @@ def tile_rbm_w_kernel(tc, input_data, W_words, W_scales, U, h_bias, y_bias, out)
         nc.scalar.dma_start(out=rows_bf[0:TILES, 0:P], in_=h_bias.rearrange("o (t p) -> (o t) p", p=P))
         nc.scalar.dma_start(out=rows_bf[0:TILES, P:], in_=U.rearrange("(t p) c -> t (p c)", p=P))
         y_sb = keep.tile([P, CLASSES], BF16)
-        nc.scalar.dma_start(out=y_sb[:], in_=y_bias.rearrange("o c -> (o c)").partition_broadcast(P))
+        nc.vector.memset(y_sb[:], 0.0)
+        nc.scalar.dma_start(out=y_sb[0:1, :], in_=y_bias)
 
         ident = keep.tile([P, P], F32)
         make_identity(nc, ident[:])
-        ones = keep.tile([P, P], F32)
-        nc.vector.memset(ones[:], 1.0)
+        signs = keep.tile([P, CLASSES, P], F32)
+        for c in range(CLASSES):
+            nc.vector.memset(signs[:, c, :], 1.0 - 2.0 * c)
 
         x_codes = keep.tile([P, GROUPS * BATCH], U32, align_bytes=64)
         x_scales = keep.tile([P, GROUPS * BATCH], U8, align_bytes=64)
         words = K_PASS // 2
+        grouped_chunks = []
+
+        def quantise_chunk(j):
+            cols = slice(j * X_CHUNK_GROUPS * BATCH, (j + 1) * X_CHUNK_GROUPS * BATCH)
+            nc.vector.quantize_mx(
+                out=x_codes[:, cols].bitcast(FP8X4), scales=x_scales[:, cols], in_=grouped_chunks[j][:]
+            )
+
         for j, x_sb in enumerate(x_chunks):
             x_words = x_sb[:].bitcast(F32)
             grouped = keep.tile([P, chunk_cols], BF16, name="grouped%d" % j, align_bytes=64)
+            grouped_chunks.append(grouped)
             for h in range(X_CHUNK_GROUPS // BANK_GROUPS):
                 turned = psum.tile([P, BANK_GROUPS, 2, BATCH], F32, tag="bank")
                 for g in range(BANK_GROUPS):
@@ -106,8 +121,9 @@ def tile_rbm_w_kernel(tc, input_data, W_words, W_scales, U, h_bias, y_bias, out)
                     nc.vector.tensor_copy(out=dst, in_=src)
                 else:
                     nc.scalar.copy(out=dst, in_=src)
-            cols = slice(j * X_CHUNK_GROUPS * BATCH, (j + 1) * X_CHUNK_GROUPS * BATCH)
-            nc.vector.quantize_mx(out=x_codes[:, cols].bitcast(FP8X4), scales=x_scales[:, cols], in_=grouped[:])
+            if j > 0:
+                quantise_chunk(j - 1)
+        quantise_chunk(len(x_chunks) - 1)
 
         u_rows = rows_bf[:, P:].rearrange("r (p c) -> r p c", c=CLASSES)
         rows = keep.tile([P, 1 + CLASSES, P], F32)
@@ -119,14 +135,15 @@ def tile_rbm_w_kernel(tc, input_data, W_words, W_scales, U, h_bias, y_bias, out)
             nc.tensor.transpose(rows_turned[:, i, :], rows[:, i, :], ident[:])
         per_unit = keep.tile([P, 1 + CLASSES, TILES], F32)
         nc.vector.tensor_copy(out=per_unit[:], in_=rows_turned[:, :, 0:TILES])
-        y_diff = keep.tile([P, CLASSES], F32)
-        for c in range(CLASSES):
-            nc.vector.tensor_sub(out=y_diff[:, c : c + 1], in0=y_sb[:, c : c + 1], in1=y_sb[:, 1 - c : 2 - c])
+        y_diff = keep.tile([P, 1], F32)
+        nc.vector.tensor_sub(out=y_diff[:], in0=y_sb[:, 0:1], in1=y_sb[:, 1:2])
 
         factors = keep.tile([P, CLASSES, BATCH], F32)
         nc.vector.memset(factors[:], 1.0)
         relu2 = keep.tile([P, BATCH], F32)
-        nc.vector.memset(relu2[:], 0.0)
+        nc.vector.tensor_scalar(
+            out=relu2[:], in0=signs[:, 0, :], scalar1=y_diff[:, 0:1], scalar2=2.0, op0=ALU.mult, op1=ALU.mult
+        )
 
         first_tile = 0
         for r, tiles in enumerate(RANGE_TILES):
@@ -176,17 +193,11 @@ def tile_rbm_w_kernel(tc, input_data, W_words, W_scales, U, h_bias, y_bias, out)
         nc.vector.scalar_tensor_tensor(
             out=partial[:], in0=relu2[:], scalar=0.5, in1=log_diff[:], op0=ALU.mult, op1=ALU.add
         )
-        logit_diff = psum.tile([P, BATCH], F32, tag="bank")
-        nc.tensor.matmul(out=logit_diff[:], lhsT=ones[:], rhs=partial[:], start=True, stop=True)
-        probs = keep.tile([P, BATCH, CLASSES], F32)
+        logit_diff = psum.tile([P, CLASSES, BATCH], F32, tag="bank")
         for c in range(CLASSES):
-            nc.scalar.activation(
-                out=probs[:, :, c],
-                in_=logit_diff[:],
-                func=ACT.Sigmoid,
-                bias=y_diff[:, c : c + 1],
-                scale=1.0 - 2.0 * c,
-            )
+            nc.tensor.matmul(out=logit_diff[:, c, :], lhsT=signs[:, c, :], rhs=partial[:], start=True, stop=True)
+        probs = keep.tile([P, BATCH, CLASSES], F32)
+        nc.scalar.activation(out=probs[:], in_=logit_diff[:].rearrange("p c b -> p b c"), func=ACT.Sigmoid)
         nc.sync.dma_start(
             out=out.rearrange("(o b) c -> o (b c)", o=1), in_=probs[0:1, :, :].rearrange("o b c -> o (b c)")
         )

@@ -51,8 +51,7 @@ def tile_rbm_w_kernel(tc, input_data, W_words, W_scales, U, h_bias, y_bias, out)
 
         w_planes = keep.tile([P, GROUPS // PLANES, HIDDEN], U8, align_bytes=64)
         nc.vector.memset(w_planes[:].rearrange("p a n -> p (a n)").bitcast(I32), 0)
-
-        def load_scale_block(a):
+        for a in range(GROUPS // PLANES):
             for q in range(QUADRANTS):
                 nc.sync.dma_start(
                     out=w_planes[32 * q : 32 * q + 4 * PLANES, a, :].bitcast(I32),
@@ -66,8 +65,6 @@ def tile_rbm_w_kernel(tc, input_data, W_words, W_scales, U, h_bias, y_bias, out)
             byte1 = (first_tile + tiles) * P * PACK
             loads = []
             for l in range(GROUPS // GROUPS_PER_LOAD):
-                if r == 0 and (l * GROUPS_PER_LOAD) % PLANES == 0:
-                    load_scale_block(l * GROUPS_PER_LOAD // PLANES)
                 w_sb = keep.tile([P, GROUPS_PER_LOAD, tiles * P], U32, name="w_sb%d_%d" % (r, l), align_bytes=64)
                 groups = W_words[l * GROUPS_PER_LOAD : (l + 1) * GROUPS_PER_LOAD]
                 nc.sync.dma_start(

@@ -22,6 +22,7 @@ K_PASS = P * PACK
 GROUPS = VISIBLE // K_PASS
 TILES = HIDDEN // P
 PLANES = 4
+PAIR = 2
 QUADRANTS = 4
 
 RANGE_TILES = (8, 6, 2)
@@ -159,36 +160,45 @@ def tile_rbm_w_kernel(tc, input_data, W_words, W_scales, U, h_bias, y_bias, out)
                         start=(g == 0),
                         stop=(g == GROUPS - 1),
                     )
-            for i in range(tiles):
-                t = first_tile + i
-                mag = work.tile([P, CLASSES, BATCH], F32)
-                for c in range(CLASSES):
-                    nc.scalar.activation(
-                        out=mag[:, c, :], in_=accs[i][:], func=ACT.Abs, bias=per_unit[:, c, t : t + 1], scale=1.0
-                    )
-                decay = work.tile([P, CLASSES, BATCH], F32)
+            for i in range(0, tiles, PAIR):
+                mag = work.tile([P, PAIR, CLASSES, BATCH], F32)
+                for k in range(PAIR):
+                    t = first_tile + i + k
+                    for c in range(CLASSES):
+                        nc.scalar.activation(
+                            out=mag[:, k, c, :],
+                            in_=accs[i + k][:],
+                            func=ACT.Abs,
+                            bias=per_unit[:, c, t : t + 1],
+                            scale=1.0,
+                        )
+                decay = work.tile([P, PAIR, CLASSES, BATCH], F32)
                 nc.scalar.activation(out=decay[:], in_=mag[:], func=ACT.Exp, scale=-1.0)
-                nc.vector.scalar_tensor_tensor(
-                    out=factors[:], in0=decay[:], scalar=1.0, in1=factors[:], op0=ALU.add, op1=ALU.mult
-                )
-                nc.vector.scalar_tensor_tensor(
-                    out=relu2[:],
-                    in0=mag[:, 0, :],
-                    scalar=per_unit[:, CLASSES, t : t + 1],
-                    in1=relu2[:],
-                    op0=ALU.add,
-                    op1=ALU.add,
-                )
-                nc.vector.tensor_sub(out=relu2[:], in0=relu2[:], in1=mag[:, 1, :])
+                for k in range(PAIR):
+                    t = first_tile + i + k
+                    nc.vector.scalar_tensor_tensor(
+                        out=relu2[:],
+                        in0=mag[:, k, 0, :],
+                        scalar=per_unit[:, CLASSES, t : t + 1],
+                        in1=relu2[:],
+                        op0=ALU.add,
+                        op1=ALU.add,
+                    )
+                    nc.vector.tensor_sub(out=relu2[:], in0=relu2[:], in1=mag[:, k, 1, :])
+                for k in range(PAIR):
+                    nc.vector.scalar_tensor_tensor(
+                        out=factors[:], in0=decay[:, k, :, :], scalar=1.0, in1=factors[:], op0=ALU.add, op1=ALU.mult
+                    )
             first_tile += tiles
 
-        logs = keep.tile([P, CLASSES, BATCH], F32)
-        nc.scalar.activation(out=logs[:], in_=factors[:], func=ACT.Ln)
-        log_diff = keep.tile([P, BATCH], F32)
-        nc.vector.tensor_sub(out=log_diff[:], in0=logs[:, 0, :], in1=logs[:, 1, :])
+        ratio = keep.tile([P, BATCH], F32)
+        nc.vector.reciprocal(out=ratio[:], in_=factors[:, 1, :])
+        nc.vector.tensor_mul(out=ratio[:], in0=ratio[:], in1=factors[:, 0, :])
+        log_ratio = keep.tile([P, BATCH], F32)
+        nc.scalar.activation(out=log_ratio[:], in_=ratio[:], func=ACT.Ln)
         partial = keep.tile([P, BATCH], F32)
         nc.vector.scalar_tensor_tensor(
-            out=partial[:], in0=relu2[:], scalar=0.5, in1=log_diff[:], op0=ALU.mult, op1=ALU.add
+            out=partial[:], in0=relu2[:], scalar=0.5, in1=log_ratio[:], op0=ALU.mult, op1=ALU.add
         )
         logit_diff = psum.tile([P, CLASSES, BATCH], F32, tag="bank")
         for c in range(CLASSES):

@@ -89,6 +89,8 @@ def tile_rbm_w_kernel(tc, input_data, W_words, W_scales, U, h_bias, y_bias, out)
         signs = keep.tile([P, CLASSES, P], F32)
         for c in range(CLASSES):
             nc.vector.memset(signs[:, c, :], 1.0 - 2.0 * c)
+        halves = keep.tile([P, P], F32)
+        nc.vector.memset(halves[:], 0.5)
 
         x_codes = keep.tile([P, GROUPS * BATCH], U32, align_bytes=64)
         x_scales = keep.tile([P, GROUPS * BATCH], U8, align_bytes=64)
@@ -133,15 +135,22 @@ def tile_rbm_w_kernel(tc, input_data, W_words, W_scales, U, h_bias, y_bias, out)
             nc.tensor.transpose(rows_turned[:, i, :], rows[:, i, :], ident[:])
         per_unit = keep.tile([P, 1 + CLASSES, TILES], F32)
         nc.vector.tensor_copy(out=per_unit[:], in_=rows_turned[:, :, 0:TILES])
+        u_sum = keep.tile([P, 1], F32)
+        nc.vector.reduce_sum(out=u_sum[:], in_=per_unit[:, CLASSES, :], axis=mybir.AxisListType.X)
         y_diff = keep.tile([P, 1], F32)
         nc.vector.tensor_sub(out=y_diff[:], in0=y_sb[:, 0:1], in1=y_sb[:, 1:2])
 
-        factors = keep.tile([P, CLASSES, BATCH], F32)
+        factors = keep.tile([P, PAIR, CLASSES, BATCH], F32)
         nc.vector.memset(factors[:], 1.0)
-        relu2 = keep.tile([P, BATCH], F32)
-        nc.vector.tensor_scalar(
-            out=relu2[:], in0=signs[:, 0, :], scalar1=y_diff[:, 0:1], scalar2=2.0, op0=ALU.mult, op1=ALU.mult
+        start = keep.tile([P, 1], F32)
+        nc.vector.scalar_tensor_tensor(
+            out=start[:], in0=y_diff[:], scalar=2.0, in1=u_sum[:], op0=ALU.mult, op1=ALU.add
         )
+        relu2 = keep.tile([P, PAIR, BATCH], F32)
+        nc.vector.tensor_scalar(
+            out=relu2[:, 0, :], in0=signs[:, 0, :], scalar1=start[:, 0:1], scalar2=None, op0=ALU.mult
+        )
+        nc.vector.memset(relu2[:, 1, :], 0.0)
 
         first_tile = 0
         for r, tiles in enumerate(RANGE_TILES):
@@ -174,37 +183,35 @@ def tile_rbm_w_kernel(tc, input_data, W_words, W_scales, U, h_bias, y_bias, out)
                         )
                 decay = work.tile([P, PAIR, CLASSES, BATCH], F32)
                 nc.scalar.activation(out=decay[:], in_=mag[:], func=ACT.Exp, scale=-1.0)
-                for k in range(PAIR):
-                    t = first_tile + i + k
+                diff = work.tile([P, PAIR, BATCH], F32)
+                nc.vector.tensor_sub(out=diff[:], in0=mag[:, :, 0, :], in1=mag[:, :, 1, :])
+                if first_tile + i + PAIR < TILES:
                     nc.vector.scalar_tensor_tensor(
-                        out=relu2[:],
-                        in0=mag[:, k, 0, :],
-                        scalar=per_unit[:, CLASSES, t : t + 1],
-                        in1=relu2[:],
-                        op0=ALU.add,
-                        op1=ALU.add,
+                        out=factors[:], in0=decay[:], scalar=1.0, in1=factors[:], op0=ALU.add, op1=ALU.mult
                     )
-                    nc.vector.tensor_sub(out=relu2[:], in0=relu2[:], in1=mag[:, k, 1, :])
-                for k in range(PAIR):
-                    nc.vector.scalar_tensor_tensor(
-                        out=factors[:], in0=decay[:, k, :, :], scalar=1.0, in1=factors[:], op0=ALU.add, op1=ALU.mult
-                    )
+                    nc.vector.tensor_add(out=relu2[:], in0=relu2[:], in1=diff[:])
             first_tile += tiles
+            if first_tile + PAIR == TILES:
+                product = keep.tile([P, CLASSES, BATCH], F32)
+                nc.vector.tensor_mul(out=product[:], in0=factors[:, 0, :, :], in1=factors[:, 1, :, :])
+                total = keep.tile([P, BATCH], F32)
+                nc.vector.tensor_add(out=total[:], in0=relu2[:, 0, :], in1=relu2[:, 1, :])
 
-        ratio = keep.tile([P, BATCH], F32)
-        nc.vector.reciprocal(out=ratio[:], in_=factors[:, 1, :])
-        nc.vector.tensor_mul(out=ratio[:], in0=ratio[:], in1=factors[:, 0, :])
-        log_ratio = keep.tile([P, BATCH], F32)
-        nc.scalar.activation(out=log_ratio[:], in_=ratio[:], func=ACT.Ln)
-        partial = keep.tile([P, BATCH], F32)
-        nc.vector.scalar_tensor_tensor(
-            out=partial[:], in0=relu2[:], scalar=0.5, in1=log_ratio[:], op0=ALU.mult, op1=ALU.add
-        )
-        logit_diff = psum.tile([P, CLASSES, BATCH], F32, tag="bank")
+        for k in range(PAIR):
+            nc.vector.scalar_tensor_tensor(
+                out=product[:], in0=decay[:, k, :, :], scalar=1.0, in1=product[:], op0=ALU.add, op1=ALU.mult
+            )
+        for k in range(PAIR):
+            nc.vector.tensor_add(out=total[:], in0=total[:], in1=diff[:, k, :])
+        logs = keep.tile([P, CLASSES, BATCH], F32)
+        nc.scalar.activation(out=logs[:], in_=product[:], func=ACT.Ln)
+        logit_diff = psum.tile([P, BATCH], F32, tag="bank")
+        nc.tensor.matmul(out=logit_diff[:], lhsT=halves[:], rhs=total[:], start=True, stop=False)
+        nc.tensor.matmul(out=logit_diff[:], lhsT=signs[:, 0, :], rhs=logs[:, 0, :], start=False, stop=False)
+        nc.tensor.matmul(out=logit_diff[:], lhsT=signs[:, 1, :], rhs=logs[:, 1, :], start=False, stop=True)
+        probs = keep.tile([1, BATCH, CLASSES], F32)
         for c in range(CLASSES):
-            nc.tensor.matmul(out=logit_diff[:, c, :], lhsT=signs[:, c, :], rhs=partial[:], start=True, stop=True)
-        probs = keep.tile([P, BATCH, CLASSES], F32)
-        nc.scalar.activation(out=probs[:], in_=logit_diff[:].rearrange("p c b -> p b c"), func=ACT.Sigmoid)
+            nc.scalar.activation(out=probs[:, :, c], in_=logit_diff[0:1, :], func=ACT.Sigmoid, scale=1.0 - 2.0 * c)
         nc.sync.dma_start(
-            out=out.rearrange("(o b) c -> o (b c)", o=1), in_=probs[0:1, :, :].rearrange("o b c -> o (b c)")
+            out=out.rearrange("(o b) c -> o (b c)", o=1), in_=probs[:].rearrange("o b c -> o (b c)")
         )

@@ -25,8 +25,9 @@ PLANES = 4
 PAIR = 2
 QUADRANTS = 4
 
-RANGE_TILES = (8, 6, 2)
+RANGE_TILES = (8, 5, 3)
 GROUPS_PER_LOAD = 2
+JOINT_GROUPS = 10
 X_CHUNK_GROUPS = 4
 BANK_GROUPS = 2
 
@@ -59,22 +60,33 @@ def tile_rbm_w_kernel(tc, input_data, W_words, W_scales, U, h_bias, y_bias, out)
                     in_=W_scales[PLANES * a : PLANES * (a + 1), 4 * q : 4 * q + 4, :].bitcast(I32),
                 )
 
-        w_loads = []
-        first_tile = 0
-        for r, tiles in enumerate(RANGE_TILES):
+        w_codes = {}
+
+        def load_weight(g0, first_tile, tiles):
+            w_sb = keep.tile(
+                [P, GROUPS_PER_LOAD, tiles * P], U32, name="w_sb%d_%d" % (g0, first_tile), align_bytes=64
+            )
             byte0 = first_tile * P * PACK
             byte1 = (first_tile + tiles) * P * PACK
-            loads = []
-            for l in range(GROUPS // GROUPS_PER_LOAD):
-                w_sb = keep.tile([P, GROUPS_PER_LOAD, tiles * P], U32, name="w_sb%d_%d" % (r, l), align_bytes=64)
-                groups = W_words[l * GROUPS_PER_LOAD : (l + 1) * GROUPS_PER_LOAD]
-                nc.sync.dma_start(
-                    out=w_sb[:].bitcast(I32),
-                    in_=groups.rearrange("g p n t -> p g (n t)")[:, :, byte0:byte1].bitcast(I32),
-                )
-                loads.append(w_sb)
-            w_loads.append(loads)
+            groups = W_words[g0 : g0 + GROUPS_PER_LOAD]
+            nc.sync.dma_start(
+                out=w_sb[:].bitcast(I32),
+                in_=groups.rearrange("g p n t -> p g (n t)")[:, :, byte0:byte1].bitcast(I32),
+            )
+            for g in range(GROUPS_PER_LOAD):
+                for i in range(tiles):
+                    w_codes[g0 + g, first_tile + i] = w_sb[:, g, i * P : (i + 1) * P]
+
+        first_tile = 0
+        for tiles in RANGE_TILES[:-1]:
+            for g in range(0, GROUPS, GROUPS_PER_LOAD):
+                load_weight(g, first_tile, tiles)
             first_tile += tiles
+        for g in range(0, JOINT_GROUPS, GROUPS_PER_LOAD):
+            load_weight(g, first_tile, RANGE_TILES[-1])
+        for t in range(first_tile, TILES):
+            for g in range(JOINT_GROUPS, GROUPS, GROUPS_PER_LOAD):
+                load_weight(g, t, 1)
 
         rows_bf = keep.tile([P, (1 + CLASSES) * P], BF16)
         nc.vector.memset(rows_bf[:], 0.0)
@@ -136,15 +148,30 @@ def tile_rbm_w_kernel(tc, input_data, W_words, W_scales, U, h_bias, y_bias, out)
         per_unit = keep.tile([P, 1 + CLASSES, TILES], F32)
         nc.vector.tensor_copy(out=per_unit[:], in_=rows_turned[:, :, 0:TILES])
         u_sum = keep.tile([P, 1], F32)
-        nc.vector.reduce_sum(out=u_sum[:], in_=per_unit[:, CLASSES, :], axis=mybir.AxisListType.X)
+        nc.vector.reduce_sum(out=u_sum[:], in_=per_unit[:, CLASSES, 0 : TILES - 1], axis=mybir.AxisListType.X)
+        b_last = per_unit[:, 0:CLASSES, TILES - 1]
+        half_bias = keep.tile([P, CLASSES], F32)
+        nc.vector.tensor_scalar(out=half_bias[:], in0=b_last, scalar1=0.5, scalar2=None, op0=ALU.mult)
+        minus_b = keep.tile([P, CLASSES], F32)
+        nc.vector.tensor_scalar(out=minus_b[:], in0=b_last, scalar1=-1.0, scalar2=None, op0=ALU.mult)
+        low = keep.tile([P, 1], F32)
+        nc.vector.tensor_tensor(out=low[:], in0=minus_b[:, 0:1], in1=minus_b[:, 1:2], op=ALU.min)
+        high = keep.tile([P, 1], F32)
+        nc.vector.tensor_tensor(out=high[:], in0=minus_b[:, 0:1], in1=minus_b[:, 1:2], op=ALU.max)
+        sign = keep.tile([P, 1], F32)
+        nc.vector.tensor_tensor(out=sign[:], in0=minus_b[:, 0:1], in1=minus_b[:, 1:2], op=ALU.is_le)
+        nc.vector.tensor_scalar(out=sign[:], in0=sign[:], scalar1=2.0, scalar2=-1.0, op0=ALU.mult, op1=ALU.add)
+        sign_low = keep.tile([P, 1], F32)
+        nc.vector.tensor_mul(out=sign_low[:], in0=sign[:], in1=low[:])
         y_diff = keep.tile([P, 1], F32)
         nc.vector.tensor_sub(out=y_diff[:], in0=y_sb[:, 0:1], in1=y_sb[:, 1:2])
 
         factors = keep.tile([P, PAIR, CLASSES, BATCH], F32)
         nc.vector.memset(factors[:], 1.0)
         start = keep.tile([P, 1], F32)
+        nc.vector.tensor_sub(out=start[:], in0=y_diff[:], in1=sign_low[:])
         nc.vector.scalar_tensor_tensor(
-            out=start[:], in0=y_diff[:], scalar=2.0, in1=u_sum[:], op0=ALU.mult, op1=ALU.add
+            out=start[:], in0=start[:], scalar=2.0, in1=u_sum[:], op0=ALU.mult, op1=ALU.add
         )
         relu2 = keep.tile([P, PAIR, BATCH], F32)
         nc.vector.tensor_scalar(
@@ -152,61 +179,98 @@ def tile_rbm_w_kernel(tc, input_data, W_words, W_scales, U, h_bias, y_bias, out)
         )
         nc.vector.memset(relu2[:, 1, :], 0.0)
 
+        accs = {}
+
+        def multiply(g, t):
+            if g == 0:
+                accs[t] = psum.tile([P, BATCH], F32, tag="bank", name="acc%d" % t)
+            plane_start = 4 * (g % PLANES)
+            nc.tensor.matmul_mx(
+                out=accs[t][:],
+                lhsT=w_codes[g, t].bitcast(FP8X4),
+                lhsT_scale=w_planes[plane_start:P, g // PLANES, t * P : (t + 1) * P],
+                rhs=x_codes[:, g * BATCH : (g + 1) * BATCH].bitcast(FP8X4),
+                rhs_scale=x_scales[:, g * BATCH : (g + 1) * BATCH],
+                start=(g == 0),
+                stop=(g == GROUPS - 1),
+            )
+
+        def magnitudes(mag, t):
+            for c in range(CLASSES):
+                nc.scalar.activation(
+                    out=mag[:, c, :], in_=accs[t][:], func=ACT.Abs, bias=per_unit[:, c, t : t + 1], scale=1.0
+                )
+
         first_tile = 0
-        for r, tiles in enumerate(RANGE_TILES):
-            accs = [psum.tile([P, BATCH], F32, tag="bank", name="acc%d" % (first_tile + i)) for i in range(tiles)]
+        for tiles in RANGE_TILES[:-1]:
             for g in range(GROUPS):
-                w_sb = w_loads[r][g // GROUPS_PER_LOAD]
-                plane_start = 4 * (g % PLANES)
-                for i in range(tiles):
-                    t = first_tile + i
-                    nc.tensor.matmul_mx(
-                        out=accs[i][:],
-                        lhsT=w_sb[:, g % GROUPS_PER_LOAD, i * P : (i + 1) * P].bitcast(FP8X4),
-                        lhsT_scale=w_planes[plane_start:P, g // PLANES, t * P : (t + 1) * P],
-                        rhs=x_codes[:, g * BATCH : (g + 1) * BATCH].bitcast(FP8X4),
-                        rhs_scale=x_scales[:, g * BATCH : (g + 1) * BATCH],
-                        start=(g == 0),
-                        stop=(g == GROUPS - 1),
-                    )
-            for i in range(0, tiles, PAIR):
+                for t in range(first_tile, first_tile + tiles):
+                    multiply(g, t)
+            for t in range(first_tile, first_tile + tiles - 1, PAIR):
                 mag = work.tile([P, PAIR, CLASSES, BATCH], F32)
                 for k in range(PAIR):
-                    t = first_tile + i + k
-                    for c in range(CLASSES):
-                        nc.scalar.activation(
-                            out=mag[:, k, c, :],
-                            in_=accs[i + k][:],
-                            func=ACT.Abs,
-                            bias=per_unit[:, c, t : t + 1],
-                            scale=1.0,
-                        )
+                    magnitudes(mag[:, k, :, :], t + k)
                 decay = work.tile([P, PAIR, CLASSES, BATCH], F32)
                 nc.scalar.activation(out=decay[:], in_=mag[:], func=ACT.Exp, scale=-1.0)
                 diff = work.tile([P, PAIR, BATCH], F32)
                 nc.vector.tensor_sub(out=diff[:], in0=mag[:, :, 0, :], in1=mag[:, :, 1, :])
-                if first_tile + i + PAIR < TILES:
-                    nc.vector.scalar_tensor_tensor(
-                        out=factors[:], in0=decay[:], scalar=1.0, in1=factors[:], op0=ALU.add, op1=ALU.mult
-                    )
-                    nc.vector.tensor_add(out=relu2[:], in0=relu2[:], in1=diff[:])
+                nc.vector.scalar_tensor_tensor(
+                    out=factors[:], in0=decay[:], scalar=1.0, in1=factors[:], op0=ALU.add, op1=ALU.mult
+                )
+                nc.vector.tensor_add(out=relu2[:], in0=relu2[:], in1=diff[:])
             first_tile += tiles
-            if first_tile + PAIR == TILES:
-                product = keep.tile([P, CLASSES, BATCH], F32)
-                nc.vector.tensor_mul(out=product[:], in0=factors[:, 0, :, :], in1=factors[:, 1, :, :])
-                total = keep.tile([P, BATCH], F32)
-                nc.vector.tensor_add(out=total[:], in0=relu2[:, 0, :], in1=relu2[:, 1, :])
+        product = keep.tile([P, CLASSES, BATCH], F32)
+        nc.vector.tensor_mul(out=product[:], in0=factors[:, 0, :, :], in1=factors[:, 1, :, :])
+        total = keep.tile([P, BATCH], F32)
+        nc.vector.tensor_add(out=total[:], in0=relu2[:, 0, :], in1=relu2[:, 1, :])
 
-        for k in range(PAIR):
+        def softplus_alone(t):
+            mag = work.tile([P, CLASSES, BATCH], F32, name="mag_alone")
+            magnitudes(mag[:], t)
+            decay = work.tile([P, CLASSES, BATCH], F32, name="decay_alone")
+            nc.scalar.activation(out=decay[:], in_=mag[:], func=ACT.Exp, scale=-1.0)
+            diff = work.tile([P, BATCH], F32, name="diff_alone")
+            nc.vector.tensor_sub(out=diff[:], in0=mag[:, 0, :], in1=mag[:, 1, :])
             nc.vector.scalar_tensor_tensor(
-                out=product[:], in0=decay[:, k, :, :], scalar=1.0, in1=product[:], op0=ALU.add, op1=ALU.mult
+                out=product[:], in0=decay[:], scalar=1.0, in1=product[:], op0=ALU.add, op1=ALU.mult
             )
-        for k in range(PAIR):
-            nc.vector.tensor_add(out=total[:], in0=total[:], in1=diff[:, k, :])
+            nc.vector.tensor_add(out=total[:], in0=total[:], in1=diff[:])
+
+        softplus_alone(first_tile - 1)
+        for g in range(JOINT_GROUPS):
+            for t in range(first_tile, TILES):
+                multiply(g, t)
+        for t in range(first_tile, TILES):
+            for g in range(JOINT_GROUPS, GROUPS):
+                multiply(g, t)
+            if t < TILES - 1:
+                softplus_alone(t)
+        last = TILES - 1
+
+        tanhs = keep.tile([P, CLASSES, BATCH], F32)
+        for c in range(CLASSES):
+            nc.scalar.activation(
+                out=tanhs[:, 1 - c, :], in_=accs[last][:], func=ACT.Tanh, bias=half_bias[:, c : c + 1], scale=0.5
+            )
+        clip = keep.tile([P, BATCH], F32)
+        nc.vector.tensor_scalar(
+            out=clip[:], in0=accs[last][:], scalar1=low[:, 0:1], scalar2=high[:, 0:1], op0=ALU.max, op1=ALU.min
+        )
+        mag_tanhs = keep.tile([P, CLASSES, BATCH], F32)
+        nc.vector.scalar_tensor_tensor(
+            out=mag_tanhs[:], in0=tanhs[:], scalar=-1.0, in1=tanhs[:], op0=ALU.mult, op1=ALU.max
+        )
+        nc.vector.scalar_tensor_tensor(
+            out=product[:], in0=mag_tanhs[:], scalar=1.0, in1=product[:], op0=ALU.add, op1=ALU.mult
+        )
+
         logs = keep.tile([P, CLASSES, BATCH], F32)
         nc.scalar.activation(out=logs[:], in_=product[:], func=ACT.Ln)
         logit_diff = psum.tile([P, BATCH], F32, tag="bank")
         nc.tensor.matmul(out=logit_diff[:], lhsT=halves[:], rhs=total[:], start=True, stop=False)
+        nc.tensor.matmul(
+            out=logit_diff[:], lhsT=sign[:, 0:1].to_broadcast([P, P]), rhs=clip[:], start=False, stop=False
+        )
         nc.tensor.matmul(out=logit_diff[:], lhsT=signs[:, 0, :], rhs=logs[:, 0, :], start=False, stop=False)
         nc.tensor.matmul(out=logit_diff[:], lhsT=signs[:, 1, :], rhs=logs[:, 1, :], start=False, stop=True)
         probs = keep.tile([1, BATCH, CLASSES], F32)

from contextlib import ExitStack

import concourse.mybir as mybir
from concourse.masks import make_identity

F32 = mybir.dt.float32
BF16 = mybir.dt.bfloat16
I32 = mybir.dt.int32
U32 = mybir.dt.uint32
U8 = mybir.dt.uint8
FP8X4 = mybir.dt.float8_e4m3fn_x4
ACT = mybir.ActivationFunctionType
ALU = mybir.AluOpType

P = 128
BATCH = 128
VISIBLE = 8192
HIDDEN = 2048
CLASSES = 2
PACK = 4
K_PASS = P * PACK
GROUPS = VISIBLE // K_PASS
TILES = HIDDEN // P
PLANES = 4
PAIR = 2
QUADRANTS = 4

RANGE_TILES = (8, 5, 3)
GROUPS_PER_LOAD = 2
JOINT_GROUPS = 10
X_CHUNK_GROUPS = 4
BANK_GROUPS = 2

FLOPS = 2 * BATCH * VISIBLE * HIDDEN

assert sum(RANGE_TILES) == TILES


def tile_rbm_w_kernel(tc, input_data, W_words, W_scales, U, h_bias, y_bias, out):
    nc = tc.nc
    with ExitStack() as ctx:
        keep = ctx.enter_context(tc.tile_pool(name="keep", bufs=1))
        work = ctx.enter_context(tc.tile_pool(name="work", bufs=4))
        psum = ctx.enter_context(tc.psum_pool(name="psum", bufs=8))
        ctx.enter_context(tc.manual_schedule())

        chunk_cols = X_CHUNK_GROUPS * K_PASS
        x_chunks = []
        for j in range(GROUPS // X_CHUNK_GROUPS):
            x_sb = keep.tile([P, chunk_cols], BF16, name="x_sb%d" % j)
            nc.sync.dma_start(out=x_sb[:], in_=input_data[:, j * chunk_cols : (j + 1) * chunk_cols])
            x_chunks.append(x_sb)

        w_planes = keep.tile([P, GROUPS // PLANES, HIDDEN], U8, align_bytes=64)
        nc.vector.memset(w_planes[:].rearrange("p a n -> p (a n)").bitcast(I32), 0)
        for a in range(GROUPS // PLANES):
            for q in range(QUADRANTS):
                nc.sync.dma_start(
                    out=w_planes[32 * q : 32 * q + 4 * PLANES, a, :].bitcast(I32),
                    in_=W_scales[PLANES * a : PLANES * (a + 1), 4 * q : 4 * q + 4, :].bitcast(I32),
                )

        w_codes = {}

        def load_weight(g0, first_tile, tiles):
            w_sb = keep.tile(
                [P, GROUPS_PER_LOAD, tiles * P], U32, name="w_sb%d_%d" % (g0, first_tile), align_bytes=64
            )
            byte0 = first_tile * P * PACK
            byte1 = (first_tile + tiles) * P * PACK
            groups = W_words[g0 : g0 + GROUPS_PER_LOAD]
            nc.sync.dma_start(
                out=w_sb[:].bitcast(I32),
                in_=groups.rearrange("g p n t -> p g (n t)")[:, :, byte0:byte1].bitcast(I32),
            )
            for g in range(GROUPS_PER_LOAD):
                for i in range(tiles):
                    w_codes[g0 + g, first_tile + i] = w_sb[:, g, i * P : (i + 1) * P]

        first_tile = 0
        for tiles in RANGE_TILES[:-1]:
            for g in range(0, GROUPS, GROUPS_PER_LOAD):
                load_weight(g, first_tile, tiles)
            first_tile += tiles
        for g in range(0, JOINT_GROUPS, GROUPS_PER_LOAD):
            load_weight(g, first_tile, RANGE_TILES[-1])
        for t in range(first_tile, TILES):
            for g in range(JOINT_GROUPS, GROUPS, GROUPS_PER_LOAD):
                load_weight(g, t, 1)

        rows_bf = keep.tile([P, (1 + CLASSES) * P], BF16)
        nc.vector.memset(rows_bf[:], 0.0)
        nc.scalar.dma_start(out=rows_bf[0:TILES, 0:P], in_=h_bias.rearrange("o (t p) -> (o t) p", p=P))
        nc.scalar.dma_start(out=rows_bf[0:TILES, P:], in_=U.rearrange("(t p) c -> t (p c)", p=P))
        y_sb = keep.tile([P, CLASSES], BF16)
        nc.vector.memset(y_sb[:], 0.0)
        nc.scalar.dma_start(out=y_sb[0:1, :], in_=y_bias)

        ident = keep.tile([P, P], F32)
        make_identity(nc, ident[:])
        signs = keep.tile([P, CLASSES, P], F32)
        for c in range(CLASSES):
            nc.vector.memset(signs[:, c, :], 1.0 - 2.0 * c)
        halves = keep.tile([P, P], F32)
        nc.vector.memset(halves[:], 0.5)

        x_codes = keep.tile([P, GROUPS * BATCH], U32, align_bytes=64)
        x_scales = keep.tile([P, GROUPS * BATCH], U8, align_bytes=64)
        words = K_PASS // 2
        grouped_chunks = []

        def quantise_chunk(j):
            cols = slice(j * X_CHUNK_GROUPS * BATCH, (j + 1) * X_CHUNK_GROUPS * BATCH)
            nc.vector.quantize_mx(
                out=x_codes[:, cols].bitcast(FP8X4), scales=x_scales[:, cols], in_=grouped_chunks[j][:]
            )

        for j, x_sb in enumerate(x_chunks):
            x_words = x_sb[:].bitcast(F32)
            grouped = keep.tile([P, chunk_cols], BF16, name="grouped%d" % j, align_bytes=64)
            grouped_chunks.append(grouped)
            for h in range(X_CHUNK_GROUPS // BANK_GROUPS):
                turned = psum.tile([P, BANK_GROUPS, 2, BATCH], F32, tag="bank")
                for g in range(BANK_GROUPS):
                    word0 = (h * BANK_GROUPS + g) * words
                    for u in range(2):
                        nc.tensor.transpose(turned[:, g, u, :], x_words[:, word0 + u : word0 + words : 2], ident[:])
                half = BANK_GROUPS * words
                dst = grouped[:].bitcast(F32)[:, h * half : (h + 1) * half]
                dst = dst.rearrange("p (g b u) -> p g b u", g=BANK_GROUPS, u=2)
                src = turned[:].rearrange("p g u b -> p g b u")
                if h % 2 == 0:
                    nc.vector.tensor_copy(out=dst, in_=src)
                else:
                    nc.scalar.copy(out=dst, in_=src)
            if j > 0:
                quantise_chunk(j - 1)
        quantise_chunk(len(x_chunks) - 1)

        u_rows = rows_bf[:, P:].rearrange("r (p c) -> r p c", c=CLASSES)
        rows = keep.tile([P, 1 + CLASSES, P], F32)
        for c in range(CLASSES):
            nc.vector.tensor_tensor(out=rows[:, c, :], in0=rows_bf[:, 0:P], in1=u_rows[:, :, c], op=ALU.add)
        nc.vector.tensor_tensor(out=rows[:, CLASSES, :], in0=u_rows[:, :, 0], in1=u_rows[:, :, 1], op=ALU.subtract)
        rows_turned = psum.tile([P, 1 + CLASSES, P], F32, tag="bank")
        for i in range(1 + CLASSES):
            nc.tensor.transpose(rows_turned[:, i, :], rows[:, i, :], ident[:])
        per_unit = keep.tile([P, 1 + CLASSES, TILES], F32)
        nc.vector.tensor_copy(out=per_unit[:], in_=rows_turned[:, :, 0:TILES])
        u_sum = keep.tile([P, 1], F32)
        nc.vector.reduce_sum(out=u_sum[:], in_=per_unit[:, CLASSES, 0 : TILES - 1], axis=mybir.AxisListType.X)
        b_last = per_unit[:, 0:CLASSES, TILES - 1]
        half_bias = keep.tile([P, CLASSES], F32)
        nc.vector.tensor_scalar(out=half_bias[:], in0=b_last, scalar1=0.5, scalar2=None, op0=ALU.mult)
        minus_b = keep.tile([P, CLASSES], F32)
        nc.vector.tensor_scalar(out=minus_b[:], in0=b_last, scalar1=-1.0, scalar2=None, op0=ALU.mult)
        low = keep.tile([P, 1], F32)
        nc.vector.tensor_tensor(out=low[:], in0=minus_b[:, 0:1], in1=minus_b[:, 1:2], op=ALU.min)
        high = keep.tile([P, 1], F32)
        nc.vector.tensor_tensor(out=high[:], in0=minus_b[:, 0:1], in1=minus_b[:, 1:2], op=ALU.max)
        sign = keep.tile([P, 1], F32)
        nc.vector.tensor_tensor(out=sign[:], in0=minus_b[:, 0:1], in1=minus_b[:, 1:2], op=ALU.is_le)
        nc.vector.tensor_scalar(out=sign[:], in0=sign[:], scalar1=2.0, scalar2=-1.0, op0=ALU.mult, op1=ALU.add)
        sign_low = keep.tile([P, 1], F32)
        nc.vector.tensor_mul(out=sign_low[:], in0=sign[:], in1=low[:])
        y_diff = keep.tile([P, 1], F32)
        nc.vector.tensor_sub(out=y_diff[:], in0=y_sb[:, 0:1], in1=y_sb[:, 1:2])

        factors = keep.tile([P, PAIR, CLASSES, BATCH], F32)
        nc.vector.memset(factors[:], 1.0)
        start = keep.tile([P, 1], F32)
        nc.vector.tensor_sub(out=start[:], in0=y_diff[:], in1=sign_low[:])
        nc.vector.scalar_tensor_tensor(
            out=start[:], in0=start[:], scalar=2.0, in1=u_sum[:], op0=ALU.mult, op1=ALU.add
        )
        relu2 = keep.tile([P, PAIR, BATCH], F32)
        nc.vector.tensor_scalar(
            out=relu2[:, 0, :], in0=signs[:, 0, :], scalar1=start[:, 0:1], scalar2=None, op0=ALU.mult
        )
        nc.vector.memset(relu2[:, 1, :], 0.0)

        accs = {}

        def multiply(g, t):
            if g == 0:
                accs[t] = psum.tile([P, BATCH], F32, tag="bank", name="acc%d" % t)
            plane_start = 4 * (g % PLANES)
            nc.tensor.matmul_mx(
                out=accs[t][:],
                lhsT=w_codes[g, t].bitcast(FP8X4),
                lhsT_scale=w_planes[plane_start:P, g // PLANES, t * P : (t + 1) * P],
                rhs=x_codes[:, g * BATCH : (g + 1) * BATCH].bitcast(FP8X4),
                rhs_scale=x_scales[:, g * BATCH : (g + 1) * BATCH],
                start=(g == 0),
                stop=(g == GROUPS - 1),
            )

        def magnitudes(mag, t):
            for c in range(CLASSES):
                nc.scalar.activation(
                    out=mag[:, c, :], in_=accs[t][:], func=ACT.Abs, bias=per_unit[:, c, t : t + 1], scale=1.0
                )

        first_tile = 0
        for tiles in RANGE_TILES[:-1]:
            for g in range(GROUPS):
                for t in range(first_tile, first_tile + tiles):
                    multiply(g, t)
            for t in range(first_tile, first_tile + tiles - 1, PAIR):
                mag = work.tile([P, PAIR, CLASSES, BATCH], F32)
                for k in range(PAIR):
                    magnitudes(mag[:, k, :, :], t + k)
                decay = work.tile([P, PAIR, CLASSES, BATCH], F32)
                nc.scalar.activation(out=decay[:], in_=mag[:], func=ACT.Exp, scale=-1.0)
                diff = work.tile([P, PAIR, BATCH], F32)
                nc.vector.tensor_sub(out=diff[:], in0=mag[:, :, 0, :], in1=mag[:, :, 1, :])
                nc.vector.scalar_tensor_tensor(
                    out=factors[:], in0=decay[:], scalar=1.0, in1=factors[:], op0=ALU.add, op1=ALU.mult
                )
                nc.vector.tensor_add(out=relu2[:], in0=relu2[:], in1=diff[:])
            first_tile += tiles
        product = keep.tile([P, CLASSES, BATCH], F32)
        nc.vector.tensor_mul(out=product[:], in0=factors[:, 0, :, :], in1=factors[:, 1, :, :])
        total = keep.tile([P, BATCH], F32)
        nc.vector.tensor_add(out=total[:], in0=relu2[:, 0, :], in1=relu2[:, 1, :])

        def softplus_alone(t):
            mag = work.tile([P, CLASSES, BATCH], F32, name="mag_alone")
            magnitudes(mag[:], t)
            decay = work.tile([P, CLASSES, BATCH], F32, name="decay_alone")
            nc.scalar.activation(out=decay[:], in_=mag[:], func=ACT.Exp, scale=-1.0)
            diff = work.tile([P, BATCH], F32, name="diff_alone")
            nc.vector.tensor_sub(out=diff[:], in0=mag[:, 0, :], in1=mag[:, 1, :])
            nc.vector.scalar_tensor_tensor(
                out=product[:], in0=decay[:], scalar=1.0, in1=product[:], op0=ALU.add, op1=ALU.mult
            )
            nc.vector.tensor_add(out=total[:], in0=total[:], in1=diff[:])

        softplus_alone(first_tile - 1)
        for g in range(JOINT_GROUPS):
            for t in range(first_tile, TILES):
                multiply(g, t)
        for t in range(first_tile, TILES):
            for g in range(JOINT_GROUPS, GROUPS):
                multiply(g, t)
            if t < TILES - 1:
                softplus_alone(t)
        last = TILES - 1

        tanhs = keep.tile([P, CLASSES, BATCH], F32)
        for c in range(CLASSES):
            nc.scalar.activation(
                out=tanhs[:, 1 - c, :], in_=accs[last][:], func=ACT.Tanh, bias=half_bias[:, c : c + 1], scale=0.5
            )
        clip = keep.tile([P, BATCH], F32)
        nc.vector.tensor_scalar(
            out=clip[:], in0=accs[last][:], scalar1=low[:, 0:1], scalar2=high[:, 0:1], op0=ALU.max, op1=ALU.min
        )
        mag_tanhs = keep.tile([P, CLASSES, BATCH], F32)
        nc.vector.scalar_tensor_tensor(
            out=mag_tanhs[:], in0=tanhs[:], scalar=-1.0, in1=tanhs[:], op0=ALU.mult, op1=ALU.max
        )
        nc.vector.scalar_tensor_tensor(
            out=product[:], in0=mag_tanhs[:], scalar=1.0, in1=product[:], op0=ALU.add, op1=ALU.mult
        )

        logs = keep.tile([P, CLASSES, BATCH], F32)
        nc.scalar.activation(out=logs[:], in_=product[:], func=ACT.Ln)
        logit_diff = psum.tile([P, BATCH], F32, tag="bank")
        nc.tensor.matmul(out=logit_diff[:], lhsT=halves[:], rhs=total[:], start=True, stop=False)
        nc.tensor.matmul(
            out=logit_diff[:], lhsT=sign[:, 0:1].to_broadcast([P, P]), rhs=clip[:], start=False, stop=False
        )
        nc.tensor.matmul(out=logit_diff[:], lhsT=signs[:, 0, :], rhs=logs[:, 0, :], start=False, stop=False)
        nc.tensor.matmul(out=logit_diff[:], lhsT=signs[:, 1, :], rhs=logs[:, 1, :], start=False, stop=True)
        probs = keep.tile([1, BATCH, CLASSES], F32)
        for c in range(CLASSES):
            nc.scalar.activation(out=probs[:, :, c], in_=logit_diff[0:1, :], func=ACT.Sigmoid, scale=1.0 - 2.0 * c)
        nc.sync.dma_start(
            out=out.rearrange("(o b) c -> o (b c)", o=1), in_=probs[:].rearrange("o b c -> o (b c)")
        )
